import numpy as np
import ml_dtypes


def mxq(x, axis, fmt="e4m3"):
    dtype, down = {"e4m3": (ml_dtypes.float8_e4m3fn, 7), "e5m2": (ml_dtypes.float8_e5m2, 14)}[fmt]
    v = np.moveaxis(np.asarray(x, np.float32).astype(ml_dtypes.bfloat16).astype(np.float64), axis, -1)
    blocks = v.reshape(v.shape[:-1] + (-1, 32))
    amax = np.abs(blocks).max(-1, keepdims=True)
    byte = np.maximum(np.where(amax > 0, np.frexp(amax)[1] - 1 + 127, 0) - down, 1)
    scale = np.exp2(byte - 127.0)
    codes = (blocks / scale).astype(np.float32).astype(dtype).astype(np.float64)
    return np.moveaxis((codes * scale).reshape(v.shape), -1, axis)


WIDE = False


def mx_kscale(k):
    if not WIDE:
        return np.ones(k)
    levels = np.array([10, -10, 5, -5, 0])
    if k % 512:
        return np.exp2(np.random.permutation(np.resize(levels, k // 32))).repeat(32)
    a = np.empty((k // 512, 16))
    for p in range(k // 512):
        a[p, :8] = np.random.permutation(np.resize(levels, 8))
        for g in range(8):
            far = levels[np.abs(levels - a[p, g]) >= 10]
            a[p, g + 8] = far[np.random.randint(len(far))]
    return np.exp2(a.ravel()).repeat(32)


BF16 = ml_dtypes.bfloat16


def bf(x):
    return np.asarray(x, np.float32).astype(BF16)


def f64(x):
    return np.asarray(x).astype(np.float64)


B, EN_MID, DE_MID = 8192, 1024, 512
K1 = EN_MID // 2
K2 = DE_MID // 2


def setup_inputs():
    s = mx_kscale(K1)
    in_data = np.random.standard_normal((B, K1, 2)) * s[None, :, None]
    return {"in_data": bf(in_data.reshape(B, EN_MID)),
            "W": bf(np.random.standard_normal((DE_MID, K1)) / np.sqrt(K1) / s[None, :]),
            "bias": bf(np.random.standard_normal(DE_MID) * 0.25)}


def reference(in_data, W, bias):
    Bsz = in_data.shape[0]
    x_imag = f64(in_data).reshape(Bsz, K1, 2)[:, :, 1]
    tmp = mxq(x_imag, 1, "e4m3") @ mxq(f64(W), 1, "e4m3").T
    act = np.maximum(tmp + f64(bias), 0.0)
    out_r = act[:, :K2] - act[:, K2:]
    out = np.stack([out_r, np.zeros_like(out_r)], axis=2)
    return out.reshape(Bsz, DE_MID, 1)

@@ -1,0 +1,213 @@
+from contextlib import ExitStack
+
+import concourse.mybir as mybir
+from concourse.masks import make_identity
+
+F32 = mybir.dt.float32
+BF16 = mybir.dt.bfloat16
+U32 = mybir.dt.uint32
+U8 = mybir.dt.uint8
+FP8X4 = mybir.dt.float8_e4m3fn_x4
+ALU = mybir.AluOpType
+ACT = mybir.ActivationFunctionType
+
+P = 128
+B = 8192
+K = 512
+N = 512
+HALF = N // 2
+PACK = 4
+FLOPS = 2 * B * K * N
+BYTES = B * K * 2 + N * K * 2 + N * 2 + B * N * 4
+
+GROUPS = [1, 1, 2] + [4] * 14 + [2, 1, 1]
+TMAX = 4
+NX = 6
+NR = 2
+ACC_BANKS = 4
+
+
+def tile_middlelayer_t_kernel(tc, in_data, W, bias, out):
+    nc = tc.nc
+    ng = len(GROUPS)
+    assert sum(GROUPS) * P == B
+    base = [P * sum(GROUPS[:g]) for g in range(ng)]
+
+    with ExitStack() as ctx:
+        ctx.enter_context(tc.manual_schedule())
+        const = ctx.enter_context(tc.tile_pool(name="const", bufs=1))
+        xpool = ctx.enter_context(tc.tile_pool(name="xpool", bufs=NX))
+        gpool = ctx.enter_context(tc.tile_pool(name="gpool", bufs=3))
+        qpool = ctx.enter_context(tc.tile_pool(name="qpool", bufs=3))
+        tpool = ctx.enter_context(tc.tile_pool(name="tpool", bufs=3))
+        opool = ctx.enter_context(tc.tile_pool(name="opool", bufs=4))
+        psum_t = ctx.enter_context(tc.psum_pool(name="psum_t", bufs=4))
+        psum_a = ctx.enter_context(tc.psum_pool(name="psum_a", bufs=ACC_BANKS))
+
+        xs = {}
+        xts = {}
+        grps = {}
+        cods = {}
+        scls = {}
+        accs = {}
+        tss = {}
+
+        def load(g):
+            tg = GROUPS[g]
+            x_sb = xpool.tile([P, tg * 2 * K], BF16, tag="x")
+            rows = in_data[base[g] : base[g] + P * tg, :]
+            nc.scalar.dma_start(out=x_sb[:], in_=rows.rearrange("(p t) c -> p (t c)", t=tg))
+            xs[g] = x_sb
+
+        b_row = const.tile([P, N], BF16)
+        nc.vector.memset(b_row[:], 0.0)
+        nc.sync.dma_start(out=b_row[0:1, :], in_=bias.rearrange("(o n) -> o n", o=1))
+        w_sb = const.tile([P, 4, K], BF16)
+        nc.scalar.dma_start(out=w_sb[:], in_=W.rearrange("(c p) k -> p c k", p=P))
+        for g in range(min(NX, ng)):
+            load(g)
+
+        ones = const.tile([P, P], BF16)
+        nc.vector.memset(ones[:], 1.0)
+        ident_b = const.tile([P, P], BF16)
+        make_identity(nc, ident_b[:])
+        ident_f = const.tile([P, P], F32)
+        make_identity(nc, ident_f[:])
+        r_tiles = [const.tile([P, 2, TMAX * HALF], F32, name="r_plane%d" % i) for i in range(NR)]
+        for r_t in r_tiles:
+            nc.vector.memset(r_t[:, 1, :], 0.0)
+
+        w_grp = const.tile([P, N * PACK], BF16, align_bytes=64)
+        w_codes = const.tile([P, N], U32, align_bytes=64)
+        w_scales = const.tile([P, N], U8, align_bytes=64)
+        for h in range(2):
+            wt = psum_t.tile([P, PACK, 2 * P], BF16, tag="xt")
+            for cc in range(2):
+                for u in range(PACK):
+                    nc.tensor.transpose(
+                        wt[:, u, cc * P : (cc + 1) * P],
+                        w_sb[:, 2 * h + cc, u:K:PACK],
+                        ident_b[:],
+                    )
+            dst = w_grp[:, h * 2 * P * PACK : (h + 1) * 2 * P * PACK].rearrange("p (n u) -> p n u", u=PACK)
+            src = wt[:].rearrange("p u n -> p n u")
+            if h == 0:
+                nc.vector.tensor_copy(out=dst, in_=src)
+            else:
+                nc.scalar.copy(out=dst, in_=src)
+        nc.vector.quantize_mx(out=w_codes[:].bitcast(FP8X4), scales=w_scales[:], in_=w_grp[:])
+
+        b_ps = psum_a.tile([P, N], F32, tag="acc")
+        nc.tensor.matmul(out=b_ps[:], lhsT=ones[:], rhs=b_row[:], start=True, stop=True)
+        bias_bc = const.tile([P, N], F32)
+        nc.vector.tensor_copy(out=bias_bc[:], in_=b_ps[:])
+
+        def transposes(g):
+            xw = xs[g][:].bitcast(F32)
+            for t in range(GROUPS[g]):
+                xt = psum_t.tile([P, PACK * P], F32, tag="xt")
+                for u in range(PACK):
+                    nc.tensor.transpose(
+                        xt[:, u * P : (u + 1) * P],
+                        xw[:, t * K + u : (t + 1) * K : PACK],
+                        ident_f[:],
+                    )
+                xts[(g, t)] = xt
+
+        def regroup(g):
+            tg = GROUPS[g]
+            grp = gpool.tile([P, tg * P * PACK], BF16, tag="grp", align_bytes=64)
+            for t in range(tg):
+                src = xts[(g, t)][:].bitcast(BF16).rearrange("p (u b e) -> p b u e", u=PACK, b=P, e=2)
+                dst = grp[:, t * P * PACK : (t + 1) * P * PACK].rearrange("p (b u) -> p b u", u=PACK)
+                nc.scalar.copy(out=dst, in_=src[:, :, :, 1])
+            grps[g] = grp
+
+        def quantise(g):
+            tg = GROUPS[g]
+            codes = qpool.tile([P, tg * P], U32, tag="codes", align_bytes=64)
+            scales = qpool.tile([P, tg * P], U8, tag="scales", align_bytes=64)
+            nc.vector.quantize_mx(out=codes[:].bitcast(FP8X4), scales=scales[:], in_=grps[g][:])
+            cods[g] = codes
+            scls[g] = scales
+
+        def multiply(g, t):
+            acc = psum_a.tile([P, N], F32, tag="acc")
+            nc.tensor.matmul_mx(
+                out=acc[:],
+                lhsT=cods[g][:, t * P : (t + 1) * P].bitcast(FP8X4),
+                lhsT_scale=scls[g][:, t * P : (t + 1) * P],
+                rhs=w_codes[:].bitcast(FP8X4),
+                rhs_scale=w_scales[:],
+                start=True,
+                stop=True,
+            )
+            accs[(g, t)] = acc
+
+        def add_bias(g, t):
+            if t == 0:
+                ts_new = tpool.tile([P, GROUPS[g], N], F32, tag="ts")
+                tss[g] = ts_new
+            nc.vector.tensor_tensor(out=tss[g][:, t, :], in0=accs[(g, t)][:], in1=bias_bc[:], op=ALU.add)
+
+        def relu_second(g):
+            v = tss[g][:, :, HALF:N]
+            nc.scalar.activation(out=v, in_=v, func=ACT.Relu)
+
+        def fold(g):
+            tg = GROUPS[g]
+            r_t = r_tiles[g % NR]
+            nc.vector.scalar_tensor_tensor(
+                out=r_t[:, 0, 0 : tg * HALF].rearrange("p (t j) -> p t j", t=tg),
+                in0=tss[g][:, :, 0:HALF],
+                scalar=0.0,
+                in1=tss[g][:, :, HALF:N],
+                op0=ALU.max,
+                op1=ALU.subtract,
+            )
+
+        def interleave_store(g):
+            tg = GROUPS[g]
+            r_t = r_tiles[g % NR]
+            o_t = opool.tile([P, tg * N], F32, tag="o")
+            cut = (tg - 1) * HALF
+            if cut:
+                nc.gpsimd.tensor_scalar(
+                    out=o_t[:, 0 : 2 * cut].rearrange("p (m e) -> p m e", e=2),
+                    in0=r_t[:, :, 0:cut].rearrange("p e m -> p m e"),
+                    scalar1=1.0,
+                    scalar2=0.0,
+                    op0=ALU.mult,
+                    op1=ALU.add,
+                )
+            nc.scalar.copy(
+                out=o_t[:, 2 * cut : tg * N].rearrange("p (m e) -> p m e", e=2),
+                in_=r_t[:, :, cut : tg * HALF].rearrange("p e m -> p m e"),
+            )
+            rows = out[base[g] : base[g] + P * tg, :, :]
+            nc.sync.dma_start(out=rows.rearrange("(p t) c o -> p (t c o)", t=tg), in_=o_t[:])
+
+        for s in range(-2, ng + 1):
+            if 0 <= s + 2 < ng:
+                transposes(s + 2)
+                regroup(s + 2)
+                if s + 2 + NX < ng:
+                    load(s + 2 + NX)
+            na = GROUPS[s] if 0 <= s < ng else 0
+            nm = GROUPS[s + 1] if 0 <= s + 1 < ng else 0
+            a_done = 0
+            m_done = 0
+            if nm:
+                quantise(s + 1)
+            while a_done < na or m_done < nm:
+                if m_done < nm and (na - a_done) + m_done < ACC_BANKS:
+                    multiply(s + 1, m_done)
+                    m_done += 1
+                else:
+                    add_bias(s, a_done)
+                    a_done += 1
+            if na:
+                relu_second(s)
+            if 0 <= s - 1 < ng:
+                fold(s - 1)
+                interleave_store(s - 1)

@@ -9,7 +9,6 @@ U32 = mybir.dt.uint32
 U8 = mybir.dt.uint8
 FP8X4 = mybir.dt.float8_e4m3fn_x4
 ALU = mybir.AluOpType
-ACT = mybir.ActivationFunctionType
 
 P = 128
 B = 8192
@@ -17,14 +16,12 @@ K = 512
 N = 512
 HALF = N // 2
 PACK = 4
+PAIR = 2
 FLOPS = 2 * B * K * N
 BYTES = B * K * 2 + N * K * 2 + N * 2 + B * N * 4
 
 GROUPS = [1, 1, 2] + [4] * 14 + [2, 1, 1]
-TMAX = 4
-NX = 6
-NR = 2
-ACC_BANKS = 4
+NX = 8
 
 
 def tile_middlelayer_t_kernel(tc, in_data, W, bias, out):
@@ -37,91 +34,104 @@ def tile_middlelayer_t_kernel(tc, in_data, W, bias, out):
         ctx.enter_context(tc.manual_schedule())
         const = ctx.enter_context(tc.tile_pool(name="const", bufs=1))
         xpool = ctx.enter_context(tc.tile_pool(name="xpool", bufs=NX))
+        ipool = ctx.enter_context(tc.tile_pool(name="ipool", bufs=3))
         gpool = ctx.enter_context(tc.tile_pool(name="gpool", bufs=3))
         qpool = ctx.enter_context(tc.tile_pool(name="qpool", bufs=3))
-        tpool = ctx.enter_context(tc.tile_pool(name="tpool", bufs=3))
-        opool = ctx.enter_context(tc.tile_pool(name="opool", bufs=4))
-        psum_t = ctx.enter_context(tc.psum_pool(name="psum_t", bufs=4))
-        psum_a = ctx.enter_context(tc.psum_pool(name="psum_a", bufs=ACC_BANKS))
+        vpool = ctx.enter_context(tc.tile_pool(name="vpool", bufs=3))
+        rpool = ctx.enter_context(tc.tile_pool(name="rpool", bufs=3))
+        opool = ctx.enter_context(tc.tile_pool(name="opool", bufs=5))
+        psum_x = ctx.enter_context(tc.psum_pool(name="psum_x", bufs=2))
+        psum_a = ctx.enter_context(tc.psum_pool(name="psum_a", bufs=4))
+        psum_o = ctx.enter_context(tc.psum_pool(name="psum_o", bufs=1))
 
         xs = {}
-        xts = {}
+        ims = {}
         grps = {}
         cods = {}
         scls = {}
-        accs = {}
-        tss = {}
+        rs = {}
 
         def load(g):
             tg = GROUPS[g]
             x_sb = xpool.tile([P, tg * 2 * K], BF16, tag="x")
             rows = in_data[base[g] : base[g] + P * tg, :]
-            nc.scalar.dma_start(out=x_sb[:], in_=rows.rearrange("(p t) c -> p (t c)", t=tg))
+            nc.sync.dma_start(out=x_sb[:], in_=rows.rearrange("(p t) c -> p (t c)", t=tg))
             xs[g] = x_sb
 
-        b_row = const.tile([P, N], BF16)
-        nc.vector.memset(b_row[:], 0.0)
-        nc.sync.dma_start(out=b_row[0:1, :], in_=bias.rearrange("(o n) -> o n", o=1))
+        b_raw = const.tile([4, P], BF16)
+        nc.scalar.dma_start(out=b_raw[:], in_=bias.rearrange("(c n) -> c n", c=4))
         w_sb = const.tile([P, 4, K], BF16)
-        nc.scalar.dma_start(out=w_sb[:], in_=W.rearrange("(c p) k -> p c k", p=P))
+        nc.sync.dma_start(out=w_sb[:], in_=W.rearrange("(c p) k -> p c k", p=P))
         for g in range(min(NX, ng)):
             load(g)
 
-        ones = const.tile([P, P], BF16)
-        nc.vector.memset(ones[:], 1.0)
-        ident_b = const.tile([P, P], BF16)
-        make_identity(nc, ident_b[:])
-        ident_f = const.tile([P, P], F32)
-        make_identity(nc, ident_f[:])
-        r_tiles = [const.tile([P, 2, TMAX * HALF], F32, name="r_plane%d" % i) for i in range(NR)]
-        for r_t in r_tiles:
-            nc.vector.memset(r_t[:, 1, :], 0.0)
+        ident = const.tile([P, P], F32)
+        make_identity(nc, ident[:])
+        zeros = const.tile([P, P], F32)
+        nc.vector.memset(zeros[:], 0.0)
+        b_rows = const.tile([P, P], F32)
+        nc.vector.memset(b_rows[:], 0.0)
+        nc.vector.tensor_copy(out=b_rows[0:4, :], in_=b_raw[:])
 
+        def extract(g):
+            tg = GROUPS[g]
+            im = ipool.tile([P, tg, K], BF16, tag="im")
+            for t in range(tg):
+                src = xs[g][:, t * 2 * K : (t + 1) * 2 * K].rearrange("p (q u e h) -> p u q e h", u=PAIR, e=2, h=2)
+                nc.gpsimd.tensor_scalar(
+                    out=im[:, t, :].rearrange("p (u q e) -> p u q e", u=PAIR, e=2),
+                    in0=src[:, :, :, :, 1],
+                    scalar1=1.0,
+                    scalar2=0.0,
+                    op0=ALU.mult,
+                    op1=ALU.add,
+                )
+            ims[g] = im
+
+        o_banks = [psum_o.tile([P, N], F32, name="o_bank%d" % i) for i in range(2)]
+        b_ps = psum_a.tile([P, N], F32, tag="acc")
+        nc.tensor.transpose(b_ps[:, 0:P], b_rows[:], ident[:])
+        nb = const.tile([P, 4], F32)
+        nc.vector.tensor_scalar(out=nb[:], in0=b_ps[:, 0:4], scalar1=-1.0, scalar2=None, op0=ALU.mult)
+        bd = const.tile([P, 2], F32)
+        nc.vector.tensor_tensor(out=bd[:], in0=nb[:, 0:2], in1=nb[:, 2:4], op=ALU.subtract)
+        for bank in o_banks:
+            for h in range(2):
+                nc.tensor.transpose(bank[:, h * HALF + 1 : (h + 1) * HALF : 2], zeros[:], ident[:])
+
+        ww = w_sb[:].rearrange("p c k -> p (c k)").bitcast(F32)
         w_grp = const.tile([P, N * PACK], BF16, align_bytes=64)
         w_codes = const.tile([P, N], U32, align_bytes=64)
         w_scales = const.tile([P, N], U8, align_bytes=64)
         for h in range(2):
-            wt = psum_t.tile([P, PACK, 2 * P], BF16, tag="xt")
+            wt = psum_x.tile([P, 2, PAIR, P], F32, tag="xt")
             for cc in range(2):
-                for u in range(PACK):
-                    nc.tensor.transpose(
-                        wt[:, u, cc * P : (cc + 1) * P],
-                        w_sb[:, 2 * h + cc, u:K:PACK],
-                        ident_b[:],
-                    )
-            dst = w_grp[:, h * 2 * P * PACK : (h + 1) * 2 * P * PACK].rearrange("p (n u) -> p n u", u=PACK)
-            src = wt[:].rearrange("p u n -> p n u")
+                off = (2 * h + cc) * (K // 2)
+                for u in range(PAIR):
+                    nc.tensor.transpose(wt[:, cc, u, :], ww[:, off + u : off + K // 2 : PAIR], ident[:])
+            dst = w_grp[:, h * HALF * PACK : (h + 1) * HALF * PACK].bitcast(F32)
+            dst = dst.rearrange("p (c n u) -> p c n u", c=2, u=PAIR)
+            src = wt[:].rearrange("p c u n -> p c n u")
             if h == 0:
                 nc.vector.tensor_copy(out=dst, in_=src)
             else:
                 nc.scalar.copy(out=dst, in_=src)
         nc.vector.quantize_mx(out=w_codes[:].bitcast(FP8X4), scales=w_scales[:], in_=w_grp[:])
 
-        b_ps = psum_a.tile([P, N], F32, tag="acc")
-        nc.tensor.matmul(out=b_ps[:], lhsT=ones[:], rhs=b_row[:], start=True, stop=True)
-        bias_bc = const.tile([P, N], F32)
-        nc.vector.tensor_copy(out=bias_bc[:], in_=b_ps[:])
-
-        def transposes(g):
-            xw = xs[g][:].bitcast(F32)
-            for t in range(GROUPS[g]):
-                xt = psum_t.tile([P, PACK * P], F32, tag="xt")
-                for u in range(PACK):
-                    nc.tensor.transpose(
-                        xt[:, u * P : (u + 1) * P],
-                        xw[:, t * K + u : (t + 1) * K : PACK],
-                        ident_f[:],
-                    )
-                xts[(g, t)] = xt
-
-        def regroup(g):
-            tg = GROUPS[g]
-            grp = gpool.tile([P, tg * P * PACK], BF16, tag="grp", align_bytes=64)
-            for t in range(tg):
-                src = xts[(g, t)][:].bitcast(BF16).rearrange("p (u b e) -> p b u e", u=PACK, b=P, e=2)
-                dst = grp[:, t * P * PACK : (t + 1) * P * PACK].rearrange("p (b u) -> p b u", u=PACK)
-                nc.scalar.copy(out=dst, in_=src[:, :, :, 1])
-            grps[g] = grp
+        def transpose_in(g, t0, nt):
+            xt = psum_x.tile([P, nt, PAIR, P], F32, tag="xt")
+            for i in range(nt):
+                words = ims[g][:, t0 + i, :].bitcast(F32)
+                for u in range(PAIR):
+                    nc.tensor.transpose(xt[:, i, u, :], words[:, u * P : (u + 1) * P], ident[:])
+            if t0 == 0:
+                grp = gpool.tile([P, GROUPS[g] * P * PACK], BF16, tag="grp", align_bytes=64)
+                grps[g] = grp
+            dst = grps[g][:, t0 * P * PACK : (t0 + nt) * P * PACK].bitcast(F32)
+            nc.scalar.copy(
+                out=dst.rearrange("p (t b u) -> p t b u", t=nt, u=PAIR),
+                in_=xt[:].rearrange("p t u b -> p t b u"),
+            )
 
         def quantise(g):
             tg = GROUPS[g]
@@ -131,83 +141,81 @@ def tile_middlelayer_t_kernel(tc, in_data, W, bias, out):
             cods[g] = codes
             scls[g] = scales
 
-        def multiply(g, t):
-            acc = psum_a.tile([P, N], F32, tag="acc")
+        def multiply(g, c):
+            acc = psum_a.tile([P, GROUPS[g] * P], F32, tag="acc")
             nc.tensor.matmul_mx(
                 out=acc[:],
-                lhsT=cods[g][:, t * P : (t + 1) * P].bitcast(FP8X4),
-                lhsT_scale=scls[g][:, t * P : (t + 1) * P],
-                rhs=w_codes[:].bitcast(FP8X4),
-                rhs_scale=w_scales[:],
+                lhsT=w_codes[:, c * P : (c + 1) * P].bitcast(FP8X4),
+                lhsT_scale=w_scales[:, c * P : (c + 1) * P],
+                rhs=cods[g][:].bitcast(FP8X4),
+                rhs_scale=scls[g][:],
                 start=True,
                 stop=True,
             )
-            accs[(g, t)] = acc
+            return acc
 
-        def add_bias(g, t):
-            if t == 0:
-                ts_new = tpool.tile([P, GROUPS[g], N], F32, tag="ts")
-                tss[g] = ts_new
-            nc.vector.tensor_tensor(out=tss[g][:, t, :], in0=accs[(g, t)][:], in1=bias_bc[:], op=ALU.add)
-
-        def relu_second(g):
-            v = tss[g][:, :, HALF:N]
-            nc.scalar.activation(out=v, in_=v, func=ACT.Relu)
-
-        def fold(g):
-            tg = GROUPS[g]
-            r_t = r_tiles[g % NR]
-            nc.vector.scalar_tensor_tensor(
-                out=r_t[:, 0, 0 : tg * HALF].rearrange("p (t j) -> p t j", t=tg),
-                in0=tss[g][:, :, 0:HALF],
-                scalar=0.0,
-                in1=tss[g][:, :, HALF:N],
-                op0=ALU.max,
-                op1=ALU.subtract,
-            )
-
-        def interleave_store(g):
-            tg = GROUPS[g]
-            r_t = r_tiles[g % NR]
-            o_t = opool.tile([P, tg * N], F32, tag="o")
-            cut = (tg - 1) * HALF
-            if cut:
-                nc.gpsimd.tensor_scalar(
-                    out=o_t[:, 0 : 2 * cut].rearrange("p (m e) -> p m e", e=2),
-                    in0=r_t[:, :, 0:cut].rearrange("p e m -> p m e"),
-                    scalar1=1.0,
-                    scalar2=0.0,
-                    op0=ALU.mult,
+        def product(g):
+            width = GROUPS[g] * P
+            r_t = rpool.tile([P, 2, width], F32, tag="r")
+            accs = [multiply(g, c) for c in (2, 0, 3, 1)]
+            for j in range(2):
+                v_t = vpool.tile([P, width], F32, tag="v")
+                nc.vector.tensor_scalar(
+                    out=v_t[:],
+                    in0=accs[2 * j][:],
+                    scalar1=nb[:, 2 + j : 3 + j],
+                    scalar2=bd[:, j : j + 1],
+                    op0=ALU.max,
                     op1=ALU.add,
                 )
-            nc.scalar.copy(
-                out=o_t[:, 2 * cut : tg * N].rearrange("p (m e) -> p m e", e=2),
-                in_=r_t[:, :, cut : tg * HALF].rearrange("p e m -> p m e"),
-            )
-            rows = out[base[g] : base[g] + P * tg, :, :]
-            nc.sync.dma_start(out=rows.rearrange("(p t) c o -> p (t c o)", t=tg), in_=o_t[:])
+                nc.vector.scalar_tensor_tensor(
+                    out=r_t[:, j, :],
+                    in0=accs[2 * j + 1][:],
+                    scalar=nb[:, j : j + 1],
+                    in1=v_t[:],
+                    op0=ALU.max,
+                    op1=ALU.subtract,
+                )
+            rs[g] = r_t
 
-        for s in range(-2, ng + 1):
-            if 0 <= s + 2 < ng:
-                transposes(s + 2)
-                regroup(s + 2)
-                if s + 2 + NX < ng:
-                    load(s + 2 + NX)
-            na = GROUPS[s] if 0 <= s < ng else 0
-            nm = GROUPS[s + 1] if 0 <= s + 1 < ng else 0
-            a_done = 0
-            m_done = 0
-            if nm:
+        turn = [0]
+        outs = {}
+
+        def transpose_out(g, t):
+            bank = o_banks[turn[0] % 2]
+            turn[0] += 1
+            for j in range(2):
+                nc.tensor.transpose(
+                    bank[:, j * HALF : (j + 1) * HALF : 2], rs[g][:, j, t * P : (t + 1) * P], ident[:]
+                )
+            if t == 0:
+                o_t = opool.tile([P, GROUPS[g], N], F32, tag="o")
+                outs[g] = o_t
+            nc.scalar.copy(out=outs[g][:, t, :], in_=bank[:])
+
+        def store(g):
+            tg = GROUPS[g]
+            rows = out[base[g] : base[g] + P * tg, :, :]
+            nc.sync.dma_start(
+                out=rows.rearrange("(p t) c o -> p (t c o)", t=tg),
+                in_=outs[g][:].rearrange("p t n -> p (t n)"),
+            )
+
+        for s in range(-3, ng + 1):
+            if 0 <= s + 3 < ng:
+                extract(s + 3)
+                if s + 3 + NX < ng:
+                    load(s + 3 + NX)
+            if 0 <= s + 1 < ng:
                 quantise(s + 1)
-            while a_done < na or m_done < nm:
-                if m_done < nm and (na - a_done) + m_done < ACC_BANKS:
-                    multiply(s + 1, m_done)
-                    m_done += 1
-                else:
-                    add_bias(s, a_done)
-                    a_done += 1
-            if na:
-                relu_second(s)
-            if 0 <= s - 1 < ng:
-                fold(s - 1)
-                interleave_store(s - 1)
+            if 0 <= s < ng:
+                product(s)
+            ti = GROUPS[s + 2] if 0 <= s + 2 < ng else 0
+            to = GROUPS[s - 1] if 0 <= s - 1 < ng else 0
+            for h in range(0, 4, 2):
+                if h < ti:
+                    transpose_in(s + 2, h, min(2, ti - h))
+                for t in range(h, min(h + 2, to)):
+                    transpose_out(s - 1, t)
+            if to:
+                store(s - 1)

@@ -40,7 +40,7 @@ def tile_middlelayer_t_kernel(tc, in_data, W, bias, out):
         vpool = ctx.enter_context(tc.tile_pool(name="vpool", bufs=3))
         rpool = ctx.enter_context(tc.tile_pool(name="rpool", bufs=3))
         opool = ctx.enter_context(tc.tile_pool(name="opool", bufs=5))
-        psum_x = ctx.enter_context(tc.psum_pool(name="psum_x", bufs=2))
+        psum_x = ctx.enter_context(tc.psum_pool(name="psum_x", bufs=1))
         psum_a = ctx.enter_context(tc.psum_pool(name="psum_a", bufs=4))
         psum_o = ctx.enter_context(tc.psum_pool(name="psum_o", bufs=1))
 
@@ -88,7 +88,7 @@ def tile_middlelayer_t_kernel(tc, in_data, W, bias, out):
                 )
             ims[g] = im
 
-        o_banks = [psum_o.tile([P, N], F32, name="o_bank%d" % i) for i in range(2)]
+        o_banks = [psum_o.tile([P, N], F32, name="o_bank%d" % i) for i in range(3)]
         b_ps = psum_a.tile([P, N], F32, tag="acc")
         nc.tensor.transpose(b_ps[:, 0:P], b_rows[:], ident[:])
         nb = const.tile([P, 4], F32)
@@ -104,7 +104,7 @@ def tile_middlelayer_t_kernel(tc, in_data, W, bias, out):
         w_codes = const.tile([P, N], U32, align_bytes=64)
         w_scales = const.tile([P, N], U8, align_bytes=64)
         for h in range(2):
-            wt = psum_x.tile([P, 2, PAIR, P], F32, tag="xt")
+            wt = psum_a.tile([P, 2, PAIR, P], F32, tag="acc")
             for cc in range(2):
                 off = (2 * h + cc) * (K // 2)
                 for u in range(PAIR):
@@ -154,35 +154,37 @@ def tile_middlelayer_t_kernel(tc, in_data, W, bias, out):
             )
             return acc
 
-        def product(g):
+        accs = {}
+
+        def fold(g, j):
             width = GROUPS[g] * P
-            r_t = rpool.tile([P, 2, width], F32, tag="r")
-            accs = [multiply(g, c) for c in (2, 0, 3, 1)]
-            for j in range(2):
-                v_t = vpool.tile([P, width], F32, tag="v")
-                nc.vector.tensor_scalar(
-                    out=v_t[:],
-                    in0=accs[2 * j][:],
-                    scalar1=nb[:, 2 + j : 3 + j],
-                    scalar2=bd[:, j : j + 1],
-                    op0=ALU.max,
-                    op1=ALU.add,
-                )
-                nc.vector.scalar_tensor_tensor(
-                    out=r_t[:, j, :],
-                    in0=accs[2 * j + 1][:],
-                    scalar=nb[:, j : j + 1],
-                    in1=v_t[:],
-                    op0=ALU.max,
-                    op1=ALU.subtract,
-                )
-            rs[g] = r_t
+            if j == 0:
+                r_t = rpool.tile([P, 2, width], F32, tag="r")
+                rs[g] = r_t
+            acc_second, acc_first = accs[g][2 * j : 2 * j + 2]
+            v_t = vpool.tile([P, width], F32, tag="v")
+            nc.vector.tensor_scalar(
+                out=v_t[:],
+                in0=acc_second[:],
+                scalar1=nb[:, 2 + j : 3 + j],
+                scalar2=bd[:, j : j + 1],
+                op0=ALU.max,
+                op1=ALU.add,
+            )
+            nc.vector.scalar_tensor_tensor(
+                out=rs[g][:, j, :],
+                in0=acc_first[:],
+                scalar=nb[:, j : j + 1],
+                in1=v_t[:],
+                op0=ALU.max,
+                op1=ALU.subtract,
+            )
 
         turn = [0]
         outs = {}
 
         def transpose_out(g, t):
-            bank = o_banks[turn[0] % 2]
+            bank = o_banks[turn[0] % len(o_banks)]
             turn[0] += 1
             for j in range(2):
                 nc.tensor.transpose(
@@ -201,21 +203,28 @@ def tile_middlelayer_t_kernel(tc, in_data, W, bias, out):
                 in_=outs[g][:].rearrange("p t n -> p (t n)"),
             )
 
-        for s in range(-3, ng + 1):
-            if 0 <= s + 3 < ng:
+        def size(g):
+            return GROUPS[g] if 0 <= g < ng else 0
+
+        for s in range(-3, ng + 2):
+            if size(s + 3):
                 extract(s + 3)
                 if s + 3 + NX < ng:
                     load(s + 3 + NX)
-            if 0 <= s + 1 < ng:
+            if size(s + 2):
+                transpose_in(s + 2, 0, min(2, size(s + 2)))
+            for t in range(2, size(s - 2)):
+                transpose_out(s - 2, t)
+            if size(s - 2):
+                store(s - 2)
+            if size(s):
+                accs[s] = [multiply(s, c) for c in (2, 0, 3, 1)]
+                fold(s, 0)
+            if size(s + 1):
                 quantise(s + 1)
-            if 0 <= s < ng:
-                product(s)
-            ti = GROUPS[s + 2] if 0 <= s + 2 < ng else 0
-            to = GROUPS[s - 1] if 0 <= s - 1 < ng else 0
-            for h in range(0, 4, 2):
-                if h < ti:
-                    transpose_in(s + 2, h, min(2, ti - h))
-                for t in range(h, min(h + 2, to)):
-                    transpose_out(s - 1, t)
-            if to:
-                store(s - 1)
+            if size(s):
+                fold(s, 1)
+            if size(s + 2) > 2:
+                transpose_in(s + 2, 2, size(s + 2) - 2)
+            for t in range(min(2, size(s - 1))):
+                transpose_out(s - 1, t)

@@ -141,8 +141,10 @@ def tile_middlelayer_t_kernel(tc, in_data, W, bias, out):
             cods[g] = codes
             scls[g] = scales
 
-        def multiply(g, c):
+        def multiply(g, c, busy):
             acc = psum_a.tile([P, GROUPS[g] * P], F32, tag="acc")
+            if busy:
+                nc.tensor.matmul(out=acc[:, 0:P], lhsT=ident[:], rhs=zeros[:], start=True, stop=True)
             nc.tensor.matmul_mx(
                 out=acc[:],
                 lhsT=w_codes[:, c * P : (c + 1) * P].bitcast(FP8X4),
@@ -211,18 +213,19 @@ def tile_middlelayer_t_kernel(tc, in_data, W, bias, out):
                 extract(s + 3)
                 if s + 3 + NX < ng:
                     load(s + 3 + NX)
+            if size(s):
+                accs[s] = [multiply(s, 2, True), multiply(s, 0, False)]
+                fold(s, 0)
             if size(s + 2):
                 transpose_in(s + 2, 0, min(2, size(s + 2)))
             for t in range(2, size(s - 2)):
                 transpose_out(s - 2, t)
             if size(s - 2):
                 store(s - 2)
-            if size(s):
-                accs[s] = [multiply(s, c) for c in (2, 0, 3, 1)]
-                fold(s, 0)
             if size(s + 1):
                 quantise(s + 1)
             if size(s):
+                accs[s] += [multiply(s, 3, True), multiply(s, 1, False)]
                 fold(s, 1)
             if size(s + 2) > 2:
                 transpose_in(s + 2, 2, size(s + 2) - 2)

@@ -97,7 +97,7 @@ def tile_middlelayer_t_kernel(tc, in_data, W, bias, out):
         nc.vector.tensor_tensor(out=bd[:], in0=nb[:, 0:2], in1=nb[:, 2:4], op=ALU.subtract)
         for bank in o_banks:
             for h in range(2):
-                nc.tensor.transpose(bank[:, h * HALF + 1 : (h + 1) * HALF : 2], zeros[:], ident[:])
+                nc.tensor.transpose(bank[:, HALF + h * P : HALF + (h + 1) * P], zeros[:], ident[:])
 
         ww = w_sb[:].rearrange("p c k -> p (c k)").bitcast(F32)
         w_grp = const.tile([P, N * PACK], BF16, align_bytes=64)
@@ -141,10 +141,8 @@ def tile_middlelayer_t_kernel(tc, in_data, W, bias, out):
             cods[g] = codes
             scls[g] = scales
 
-        def multiply(g, c, busy):
+        def multiply(g, c):
             acc = psum_a.tile([P, GROUPS[g] * P], F32, tag="acc")
-            if busy:
-                nc.tensor.matmul(out=acc[:, 0:P], lhsT=ident[:], rhs=zeros[:], start=True, stop=True)
             nc.tensor.matmul_mx(
                 out=acc[:],
                 lhsT=w_codes[:, c * P : (c + 1) * P].bitcast(FP8X4),
@@ -189,13 +187,14 @@ def tile_middlelayer_t_kernel(tc, in_data, W, bias, out):
             bank = o_banks[turn[0] % len(o_banks)]
             turn[0] += 1
             for j in range(2):
-                nc.tensor.transpose(
-                    bank[:, j * HALF : (j + 1) * HALF : 2], rs[g][:, j, t * P : (t + 1) * P], ident[:]
-                )
+                nc.tensor.transpose(bank[:, j * P : (j + 1) * P], rs[g][:, j, t * P : (t + 1) * P], ident[:])
             if t == 0:
                 o_t = opool.tile([P, GROUPS[g], N], F32, tag="o")
                 outs[g] = o_t
-            nc.scalar.copy(out=outs[g][:, t, :], in_=bank[:])
+            nc.scalar.copy(
+                out=outs[g][:, t, :].rearrange("p (m e) -> p m e", e=2),
+                in_=bank[:].rearrange("p (e m) -> p m e", e=2),
+            )
 
         def store(g):
             tg = GROUPS[g]
@@ -214,7 +213,7 @@ def tile_middlelayer_t_kernel(tc, in_data, W, bias, out):
                 if s + 3 + NX < ng:
                     load(s + 3 + NX)
             if size(s):
-                accs[s] = [multiply(s, 2, True), multiply(s, 0, False)]
+                accs[s] = [multiply(s, 2), multiply(s, 0)]
                 fold(s, 0)
             if size(s + 2):
                 transpose_in(s + 2, 0, min(2, size(s + 2)))
@@ -225,7 +224,7 @@ def tile_middlelayer_t_kernel(tc, in_data, W, bias, out):
             if size(s + 1):
                 quantise(s + 1)
             if size(s):
-                accs[s] += [multiply(s, 3, True), multiply(s, 1, False)]
+                accs[s] += [multiply(s, 3), multiply(s, 1)]
                 fold(s, 1)
             if size(s + 2) > 2:
                 transpose_in(s + 2, 2, size(s + 2) - 2)

@@ -60,8 +60,12 @@ def tile_middlelayer_t_kernel(tc, in_data, W, bias, out):
 
         b_raw = const.tile([4, P], BF16)
         nc.scalar.dma_start(out=b_raw[:], in_=bias.rearrange("(c n) -> c n", c=4))
-        w_sb = const.tile([P, 4, K], BF16)
-        nc.sync.dma_start(out=w_sb[:], in_=W.rearrange("(c p) k -> p c k", p=P))
+        w_halves = []
+        for h in range(2):
+            w_half = const.tile([P, 2, K], BF16, name="w_half%d" % h)
+            rows = W[h * HALF : (h + 1) * HALF, :]
+            nc.sync.dma_start(out=w_half[:], in_=rows.rearrange("(c p) k -> p c k", p=P))
+            w_halves.append(w_half)
         for g in range(min(NX, ng)):
             load(g)
 
@@ -73,40 +77,33 @@ def tile_middlelayer_t_kernel(tc, in_data, W, bias, out):
         nc.vector.memset(b_rows[:], 0.0)
         nc.vector.tensor_copy(out=b_rows[0:4, :], in_=b_raw[:])
 
+        def vector_tile(g):
+            return 3 if GROUPS[g] == 4 and g % 2 else None
+
+        def extract_tile(engine, g, t):
+            dst = ims[g][:, t * K : (t + 1) * K].rearrange("p (u q e) -> p u q e", u=PAIR, e=2)
+            src = xs[g][:, t * 2 * K : (t + 1) * 2 * K].rearrange("p (q u e h) -> p u q e h", u=PAIR, e=2, h=2)
+            src = src[:, :, :, :, 1]
+            if engine == "vector":
+                nc.vector.tensor_copy(out=dst, in_=src)
+            else:
+                nc.gpsimd.tensor_scalar(out=dst, in0=src, scalar1=1.0, scalar2=0.0, op0=ALU.mult, op1=ALU.add)
+
         def extract(g):
-            tg = GROUPS[g]
-            im = ipool.tile([P, tg, K], BF16, tag="im")
-            for t in range(tg):
-                src = xs[g][:, t * 2 * K : (t + 1) * 2 * K].rearrange("p (q u e h) -> p u q e h", u=PAIR, e=2, h=2)
-                nc.gpsimd.tensor_scalar(
-                    out=im[:, t, :].rearrange("p (u q e) -> p u q e", u=PAIR, e=2),
-                    in0=src[:, :, :, :, 1],
-                    scalar1=1.0,
-                    scalar2=0.0,
-                    op0=ALU.mult,
-                    op1=ALU.add,
-                )
+            im = ipool.tile([P, GROUPS[g] * K], BF16, tag="im")
             ims[g] = im
+            for t in range(GROUPS[g]):
+                if t != vector_tile(g):
+                    extract_tile("gpsimd", g, t)
 
-        o_banks = [psum_o.tile([P, N], F32, name="o_bank%d" % i) for i in range(3)]
-        b_ps = psum_a.tile([P, N], F32, tag="acc")
-        nc.tensor.transpose(b_ps[:, 0:P], b_rows[:], ident[:])
-        nb = const.tile([P, 4], F32)
-        nc.vector.tensor_scalar(out=nb[:], in0=b_ps[:, 0:4], scalar1=-1.0, scalar2=None, op0=ALU.mult)
-        bd = const.tile([P, 2], F32)
-        nc.vector.tensor_tensor(out=bd[:], in0=nb[:, 0:2], in1=nb[:, 2:4], op=ALU.subtract)
-        for bank in o_banks:
-            for h in range(2):
-                nc.tensor.transpose(bank[:, HALF + h * P : HALF + (h + 1) * P], zeros[:], ident[:])
-
-        ww = w_sb[:].rearrange("p c k -> p (c k)").bitcast(F32)
         w_grp = const.tile([P, N * PACK], BF16, align_bytes=64)
         w_codes = const.tile([P, N], U32, align_bytes=64)
         w_scales = const.tile([P, N], U8, align_bytes=64)
         for h in range(2):
+            ww = w_halves[h][:].rearrange("p c k -> p (c k)").bitcast(F32)
             wt = psum_a.tile([P, 2, PAIR, P], F32, tag="acc")
             for cc in range(2):
-                off = (2 * h + cc) * (K // 2)
+                off = cc * (K // 2)
                 for u in range(PAIR):
                     nc.tensor.transpose(wt[:, cc, u, :], ww[:, off + u : off + K // 2 : PAIR], ident[:])
             dst = w_grp[:, h * HALF * PACK : (h + 1) * HALF * PACK].bitcast(F32)
@@ -118,10 +115,23 @@ def tile_middlelayer_t_kernel(tc, in_data, W, bias, out):
                 nc.scalar.copy(out=dst, in_=src)
         nc.vector.quantize_mx(out=w_codes[:].bitcast(FP8X4), scales=w_scales[:], in_=w_grp[:])
 
+        o_banks = [psum_o.tile([P, N], F32, name="o_bank%d" % i) for i in range(3)]
+        b_ps = psum_a.tile([P, N], F32, tag="acc")
+        nc.tensor.transpose(b_ps[:, 0:P], b_rows[:], ident[:])
+        nb = const.tile([P, 4], F32)
+        nc.vector.tensor_scalar(out=nb[:], in0=b_ps[:, 0:4], scalar1=-1.0, scalar2=None, op0=ALU.mult)
+        bd = const.tile([P, 2], F32)
+        nc.vector.tensor_tensor(out=bd[:], in0=nb[:, 0:2], in1=nb[:, 2:4], op=ALU.subtract)
+
+        def zero_odd_columns():
+            for bank in o_banks:
+                for h in range(2):
+                    nc.tensor.transpose(bank[:, HALF + h * P : HALF + (h + 1) * P], zeros[:], ident[:])
+
         def transpose_in(g, t0, nt):
             xt = psum_x.tile([P, nt, PAIR, P], F32, tag="xt")
             for i in range(nt):
-                words = ims[g][:, t0 + i, :].bitcast(F32)
+                words = ims[g][:, (t0 + i) * K : (t0 + i + 1) * K].bitcast(F32)
                 for u in range(PAIR):
                     nc.tensor.transpose(xt[:, i, u, :], words[:, u * P : (u + 1) * P], ident[:])
             if t0 == 0:
@@ -208,10 +218,10 @@ def tile_middlelayer_t_kernel(tc, in_data, W, bias, out):
             return GROUPS[g] if 0 <= g < ng else 0
 
         for s in range(-3, ng + 2):
+            if s == 0:
+                zero_odd_columns()
             if size(s + 3):
                 extract(s + 3)
-                if s + 3 + NX < ng:
-                    load(s + 3 + NX)
             if size(s):
                 accs[s] = [multiply(s, 2), multiply(s, 0)]
                 fold(s, 0)
@@ -226,6 +236,10 @@ def tile_middlelayer_t_kernel(tc, in_data, W, bias, out):
             if size(s):
                 accs[s] += [multiply(s, 3), multiply(s, 1)]
                 fold(s, 1)
+            if size(s + 3) and vector_tile(s + 3) is not None:
+                extract_tile("vector", s + 3, vector_tile(s + 3))
+            if size(s + 3) and s + 3 + NX < ng:
+                load(s + 3 + NX)
             if size(s + 2) > 2:
                 transpose_in(s + 2, 2, size(s + 2) - 2)
             for t in range(min(2, size(s - 1))):

from contextlib import ExitStack

import concourse.mybir as mybir
from concourse.masks import make_identity

F32 = mybir.dt.float32
BF16 = mybir.dt.bfloat16
U32 = mybir.dt.uint32
U8 = mybir.dt.uint8
FP8X4 = mybir.dt.float8_e4m3fn_x4
ALU = mybir.AluOpType

P = 128
B = 8192
K = 512
N = 512
HALF = N // 2
PACK = 4
PAIR = 2
FLOPS = 2 * B * K * N
BYTES = B * K * 2 + N * K * 2 + N * 2 + B * N * 4

GROUPS = [1, 1, 2] + [4] * 14 + [2, 1, 1]
NX = 8


def tile_middlelayer_t_kernel(tc, in_data, W, bias, out):
    nc = tc.nc
    ng = len(GROUPS)
    assert sum(GROUPS) * P == B
    base = [P * sum(GROUPS[:g]) for g in range(ng)]

    with ExitStack() as ctx:
        ctx.enter_context(tc.manual_schedule())
        const = ctx.enter_context(tc.tile_pool(name="const", bufs=1))
        xpool = ctx.enter_context(tc.tile_pool(name="xpool", bufs=NX))
        ipool = ctx.enter_context(tc.tile_pool(name="ipool", bufs=3))
        gpool = ctx.enter_context(tc.tile_pool(name="gpool", bufs=3))
        qpool = ctx.enter_context(tc.tile_pool(name="qpool", bufs=3))
        vpool = ctx.enter_context(tc.tile_pool(name="vpool", bufs=3))
        rpool = ctx.enter_context(tc.tile_pool(name="rpool", bufs=3))
        opool = ctx.enter_context(tc.tile_pool(name="opool", bufs=5))
        psum_x = ctx.enter_context(tc.psum_pool(name="psum_x", bufs=1))
        psum_a = ctx.enter_context(tc.psum_pool(name="psum_a", bufs=4))
        psum_o = ctx.enter_context(tc.psum_pool(name="psum_o", bufs=1))

        xs = {}
        ims = {}
        grps = {}
        cods = {}
        scls = {}
        rs = {}

        def load(g):
            tg = GROUPS[g]
            x_sb = xpool.tile([P, tg * 2 * K], BF16, tag="x")
            rows = in_data[base[g] : base[g] + P * tg, :]
            nc.sync.dma_start(out=x_sb[:], in_=rows.rearrange("(p t) c -> p (t c)", t=tg))
            xs[g] = x_sb

        b_raw = const.tile([4, P], BF16)
        nc.scalar.dma_start(out=b_raw[:], in_=bias.rearrange("(c n) -> c n", c=4))
        w_halves = []
        for h in range(2):
            w_half = const.tile([P, 2, K], BF16, name="w_half%d" % h)
            rows = W[h * HALF : (h + 1) * HALF, :]
            nc.sync.dma_start(out=w_half[:], in_=rows.rearrange("(c p) k -> p c k", p=P))
            w_halves.append(w_half)
        for g in range(min(NX, ng)):
            load(g)

        ident = const.tile([P, P], F32)
        make_identity(nc, ident[:])
        zeros = const.tile([P, P], F32)
        nc.vector.memset(zeros[:], 0.0)
        b_rows = const.tile([P, P], F32)
        nc.vector.memset(b_rows[:], 0.0)
        nc.vector.tensor_copy(out=b_rows[0:4, :], in_=b_raw[:])

        def vector_tile(g):
            return 3 if GROUPS[g] == 4 and g % 2 else None

        def extract_tile(engine, g, t):
            dst = ims[g][:, t * K : (t + 1) * K].rearrange("p (u q e) -> p u q e", u=PAIR, e=2)
            src = xs[g][:, t * 2 * K : (t + 1) * 2 * K].rearrange("p (q u e h) -> p u q e h", u=PAIR, e=2, h=2)
            src = src[:, :, :, :, 1]
            if engine == "vector":
                nc.vector.tensor_copy(out=dst, in_=src)
            else:
                nc.gpsimd.tensor_scalar(out=dst, in0=src, scalar1=1.0, scalar2=0.0, op0=ALU.mult, op1=ALU.add)

        def extract(g):
            im = ipool.tile([P, GROUPS[g] * K], BF16, tag="im")
            ims[g] = im
            for t in range(GROUPS[g]):
                if t != vector_tile(g):
                    extract_tile("gpsimd", g, t)

        w_grp = const.tile([P, N * PACK], BF16, align_bytes=64)
        w_codes = const.tile([P, N], U32, align_bytes=64)
        w_scales = const.tile([P, N], U8, align_bytes=64)
        for h in range(2):
            ww = w_halves[h][:].rearrange("p c k -> p (c k)").bitcast(F32)
            wt = psum_a.tile([P, 2, PAIR, P], F32, tag="acc")
            for cc in range(2):
                off = cc * (K // 2)
                for u in range(PAIR):
                    nc.tensor.transpose(wt[:, cc, u, :], ww[:, off + u : off + K // 2 : PAIR], ident[:])
            dst = w_grp[:, h * HALF * PACK : (h + 1) * HALF * PACK].bitcast(F32)
            dst = dst.rearrange("p (c n u) -> p c n u", c=2, u=PAIR)
            src = wt[:].rearrange("p c u n -> p c n u")
            if h == 0:
                nc.vector.tensor_copy(out=dst, in_=src)
            else:
                nc.scalar.copy(out=dst, in_=src)
        nc.vector.quantize_mx(out=w_codes[:].bitcast(FP8X4), scales=w_scales[:], in_=w_grp[:])

        o_banks = [psum_o.tile([P, N], F32, name="o_bank%d" % i) for i in range(3)]
        b_ps = psum_a.tile([P, N], F32, tag="acc")
        nc.tensor.transpose(b_ps[:, 0:P], b_rows[:], ident[:])
        nb = const.tile([P, 4], F32)
        nc.vector.tensor_scalar(out=nb[:], in0=b_ps[:, 0:4], scalar1=-1.0, scalar2=None, op0=ALU.mult)
        bd = const.tile([P, 2], F32)
        nc.vector.tensor_tensor(out=bd[:], in0=nb[:, 0:2], in1=nb[:, 2:4], op=ALU.subtract)

        def zero_odd_columns():
            for bank in o_banks:
                for h in range(2):
                    nc.tensor.transpose(bank[:, HALF + h * P : HALF + (h + 1) * P], zeros[:], ident[:])

        def transpose_in(g, t0, nt):
            xt = psum_x.tile([P, nt, PAIR, P], F32, tag="xt")
            for i in range(nt):
                words = ims[g][:, (t0 + i) * K : (t0 + i + 1) * K].bitcast(F32)
                for u in range(PAIR):
                    nc.tensor.transpose(xt[:, i, u, :], words[:, u * P : (u + 1) * P], ident[:])
            if t0 == 0:
                grp = gpool.tile([P, GROUPS[g] * P * PACK], BF16, tag="grp", align_bytes=64)
                grps[g] = grp
            dst = grps[g][:, t0 * P * PACK : (t0 + nt) * P * PACK].bitcast(F32)
            nc.scalar.copy(
                out=dst.rearrange("p (t b u) -> p t b u", t=nt, u=PAIR),
                in_=xt[:].rearrange("p t u b -> p t b u"),
            )

        def quantise(g):
            tg = GROUPS[g]
            codes = qpool.tile([P, tg * P], U32, tag="codes", align_bytes=64)
            scales = qpool.tile([P, tg * P], U8, tag="scales", align_bytes=64)
            nc.vector.quantize_mx(out=codes[:].bitcast(FP8X4), scales=scales[:], in_=grps[g][:])
            cods[g] = codes
            scls[g] = scales

        def multiply(g, c):
            acc = psum_a.tile([P, GROUPS[g] * P], F32, tag="acc")
            nc.tensor.matmul_mx(
                out=acc[:],
                lhsT=w_codes[:, c * P : (c + 1) * P].bitcast(FP8X4),
                lhsT_scale=w_scales[:, c * P : (c + 1) * P],
                rhs=cods[g][:].bitcast(FP8X4),
                rhs_scale=scls[g][:],
                start=True,
                stop=True,
            )
            return acc

        accs = {}

        def fold(g, j):
            width = GROUPS[g] * P
            if j == 0:
                r_t = rpool.tile([P, 2, width], F32, tag="r")
                rs[g] = r_t
            acc_second, acc_first = accs[g][2 * j : 2 * j + 2]
            v_t = vpool.tile([P, width], F32, tag="v")
            nc.vector.tensor_scalar(
                out=v_t[:],
                in0=acc_second[:],
                scalar1=nb[:, 2 + j : 3 + j],
                scalar2=bd[:, j : j + 1],
                op0=ALU.max,
                op1=ALU.add,
            )
            nc.vector.scalar_tensor_tensor(
                out=rs[g][:, j, :],
                in0=acc_first[:],
                scalar=nb[:, j : j + 1],
                in1=v_t[:],
                op0=ALU.max,
                op1=ALU.subtract,
            )

        turn = [0]
        outs = {}

        def transpose_out(g, t):
            bank = o_banks[turn[0] % len(o_banks)]
            turn[0] += 1
            for j in range(2):
                nc.tensor.transpose(bank[:, j * P : (j + 1) * P], rs[g][:, j, t * P : (t + 1) * P], ident[:])
            if t == 0:
                o_t = opool.tile([P, GROUPS[g], N], F32, tag="o")
                outs[g] = o_t
            nc.scalar.copy(
                out=outs[g][:, t, :].rearrange("p (m e) -> p m e", e=2),
                in_=bank[:].rearrange("p (e m) -> p m e", e=2),
            )

        def store(g):
            tg = GROUPS[g]
            rows = out[base[g] : base[g] + P * tg, :, :]
            nc.sync.dma_start(
                out=rows.rearrange("(p t) c o -> p (t c o)", t=tg),
                in_=outs[g][:].rearrange("p t n -> p (t n)"),
            )

        def size(g):
            return GROUPS[g] if 0 <= g < ng else 0

        for s in range(-3, ng + 2):
            if s == 0:
                zero_odd_columns()
            if size(s + 3):
                extract(s + 3)
            if size(s):
                accs[s] = [multiply(s, 2), multiply(s, 0)]
                fold(s, 0)
            if size(s + 2):
                transpose_in(s + 2, 0, min(2, size(s + 2)))
            for t in range(2, size(s - 2)):
                transpose_out(s - 2, t)
            if size(s - 2):
                store(s - 2)
            if size(s + 1):
                quantise(s + 1)
            if size(s):
                accs[s] += [multiply(s, 3), multiply(s, 1)]
                fold(s, 1)
            if size(s + 3) and vector_tile(s + 3) is not None:
                extract_tile("vector", s + 3, vector_tile(s + 3))
            if size(s + 3) and s + 3 + NX < ng:
                load(s + 3 + NX)
            if size(s + 2) > 2:
                transpose_in(s + 2, 2, size(s + 2) - 2)
            for t in range(min(2, size(s - 1))):
                transpose_out(s - 1, t)
